import numpy as np
import ml_dtypes


def mxq(x, axis, fmt="e4m3"):
    dtype, down = {"e4m3": (ml_dtypes.float8_e4m3fn, 7), "e5m2": (ml_dtypes.float8_e5m2, 14)}[fmt]
    v = np.moveaxis(np.asarray(x, np.float32).astype(ml_dtypes.bfloat16).astype(np.float64), axis, -1)
    blocks = v.reshape(v.shape[:-1] + (-1, 32))
    amax = np.abs(blocks).max(-1, keepdims=True)
    byte = np.maximum(np.where(amax > 0, np.frexp(amax)[1] - 1 + 127, 0) - down, 1)
    scale = np.exp2(byte - 127.0)
    codes = (blocks / scale).astype(np.float32).astype(dtype).astype(np.float64)
    return np.moveaxis((codes * scale).reshape(v.shape), -1, axis)


WIDE = False


def mx_kscale(k):
    if not WIDE:
        return np.ones(k)
    levels = np.array([10, -10, 5, -5, 0])
    a = np.random.permutation(np.resize(levels, k // 512 * 4)).reshape(k // 512, 4)
    idx = np.arange(k)
    return np.exp2(a[idx // 512, idx % 128 // 32])


BF16 = ml_dtypes.bfloat16


def bf(x):
    return np.asarray(x, np.float32).astype(BF16)


def f64(x):
    return np.asarray(x).astype(np.float64)


E2M1 = np.array([0.0, 0.5, 1.0, 1.5, 2.0, 3.0, 4.0, 6.0, -0.0, -0.5, -1.0, -1.5, -2.0, -3.0, -4.0, -6.0])


def pack_weight(w, fmt):
    k, n = w.shape
    w = f64(bf(w)).reshape(k // 32, 32, n)
    amax = np.abs(w).max(1)
    if fmt == "e4m3":
        byte = np.frexp(amax)[1] - 1 + 127 - 7
    else:
        mant, ex = np.frexp(amax / 6.0)
        byte = np.where(mant > 0.5, ex, ex - 1) + 127
    byte = np.clip(np.where(amax > 0, byte, 1), 1, 254)
    scaled = (w * np.exp2(127.0 - byte)[:, None, :]).reshape(k, n).astype(np.float32)
    by_word = np.ascontiguousarray(scaled.reshape(k // 512, 128, 4, n).transpose(0, 1, 3, 2))
    if fmt == "e4m3":
        words = by_word.astype(ml_dtypes.float8_e4m3fn).view(np.uint8)
    else:
        c = by_word.astype(ml_dtypes.float4_e2m1fn).view(np.uint8) & 0xF
        words = c[..., 0::2] | (c[..., 1::2] << 4)
    return np.ascontiguousarray(words), np.ascontiguousarray(byte.astype(np.uint8).reshape(k // 512, 16, n))


def unpack_weight(words, scales, fmt):
    g, p, n, _ = words.shape
    if fmt == "e4m3":
        vals = np.ascontiguousarray(words).view(ml_dtypes.float8_e4m3fn).astype(np.float64)
    else:
        nib = np.empty((g, p, n, 4), np.uint8)
        nib[..., 0::2] = words & 0xF
        nib[..., 1::2] = words >> 4
        vals = E2M1[nib]
    vals = vals * np.repeat(np.exp2(scales.astype(np.float64) - 127.0), 8, axis=1)[..., None]
    return vals.transpose(0, 1, 3, 2).reshape(g * 512, n)


BATCH, ROWS, COLS, IN_DIM, OUT_DIM = 2, 8, 8, 16384, 1024
N = ROWS * COLS
EPS_BN = 1e-5
EPS_DEG = 1e-5
FMT = "e4m3"


def _stencil9(x):
    R, C = x.shape[-3], x.shape[-2]
    pad = [(0, 0)] * (x.ndim - 3) + [(1, 1), (1, 1), (0, 0)]
    xp = np.pad(x, pad)
    out = np.zeros_like(x)
    for di in range(3):
        for dj in range(3):
            out = out + xp[..., di:di + R, dj:dj + C, :]
    return out


def _deg_inv_sqrt(rows, cols):
    D = _stencil9(np.ones((rows, cols, 1)))[..., 0]
    return (D + EPS_DEG) ** -0.5


def setup_inputs():
    s = mx_kscale(IN_DIM)
    mu = 0.5 * np.random.standard_normal(IN_DIM)
    bound = np.sqrt(6.0 / IN_DIM)
    H = bf((np.random.standard_normal((BATCH, N, IN_DIM)) + mu) * s)
    W_words, W_scales = pack_weight(np.random.uniform(-bound, bound, (IN_DIM, OUT_DIM)) / s[:, None], FMT)
    return {"H": H,
            "W_words": W_words,
            "W_scales": W_scales,
            "gamma": bf(1.0 + 0.1 * np.random.standard_normal(OUT_DIM)),
            "beta": bf(0.2 * np.random.standard_normal(OUT_DIM))}


def reference(H, W_words, W_scales, gamma, beta):
    B, n_nodes, _ = H.shape
    Ht = mxq(f64(H), 2, "e4m3") @ unpack_weight(W_words, W_scales, FMT)
    mean = Ht.mean(axis=(0, 1))
    var = Ht.var(axis=(0, 1))
    Ht = (Ht - mean) * (1.0 / np.sqrt(var + EPS_BN)) * f64(gamma) + f64(beta)
    Ht = np.maximum(Ht, 0.0)
    d = _deg_inv_sqrt(ROWS, COLS)[None, :, :, None]
    Hg = Ht.reshape(B, ROWS, COLS, OUT_DIM)
    Hagg = d * _stencil9(Hg * d)
    return Hagg.reshape(B, n_nodes, OUT_DIM)

@@ -1,0 +1,263 @@
+from contextlib import ExitStack
+
+import concourse.masks as masks
+import concourse.mybir as mybir
+
+F32 = mybir.dt.float32
+BF16 = mybir.dt.bfloat16
+I32 = mybir.dt.int32
+U32 = mybir.dt.uint32
+U8 = mybir.dt.uint8
+FP8X4 = mybir.dt.float8_e4m3fn_x4
+ALU = mybir.AluOpType
+ACT = mybir.ActivationFunctionType
+AXIS = mybir.AxisListType
+
+P = 128
+TOKENS = 128
+K = 16384
+FEATURES = 1024
+K_PASS = 512
+GROUPS = K // K_PASS
+F_TILES = FEATURES // P
+BANKS = 8
+H_CHUNKS = 4
+GROUPS_PER_H_CHUNK = GROUPS // H_CHUNKS
+W_GROUPS_PER_LOAD = 2
+SPLIT_GROUPS = 8
+HALF = FEATURES // 2
+SPLIT_GROUPS_PER_LOAD = 2
+PLANES_PER_TILE = 4
+EPS_BN = 1e-5
+EPS_DEG = 1e-5
+
+FLOPS = 2 * TOKENS * K * FEATURES
+
+
+def build_grid_tables(nc, const, psum, ident):
+    row_int = const.tile([P, TOKENS], I32)
+    col_int = const.tile([P, TOKENS], I32)
+    nc.gpsimd.iota(row_int[:], pattern=[[9, 2], [1, 8], [0, 8]], base=0, channel_multiplier=0)
+    nc.gpsimd.iota(col_int[:], pattern=[[0, 16], [1, 8]], base=0, channel_multiplier=0)
+    row_free = const.tile([P, TOKENS], F32)
+    col_free = const.tile([P, TOKENS], F32)
+    nc.vector.tensor_copy(out=row_free[:], in_=row_int[:])
+    nc.vector.tensor_copy(out=col_free[:], in_=col_int[:])
+    row_own = psum.tile([P, TOKENS], F32, tag="bank5")
+    col_own = psum.tile([P, TOKENS], F32, tag="bank6")
+    nc.tensor.transpose(row_own[:], row_free[:], ident[:])
+    nc.tensor.transpose(col_own[:], col_free[:], ident[:])
+    row_gap = const.tile([P, TOKENS], F32)
+    col_gap = const.tile([P, TOKENS], F32)
+    nc.vector.tensor_sub(out=row_gap[:], in0=row_free[:], in1=row_own[:])
+    nc.vector.tensor_sub(out=col_gap[:], in0=col_free[:], in1=col_own[:])
+    nc.vector.tensor_mul(out=row_gap[:], in0=row_gap[:], in1=row_gap[:])
+    nc.vector.tensor_mul(out=col_gap[:], in0=col_gap[:], in1=col_gap[:])
+    dist2 = const.tile([P, TOKENS], F32)
+    nc.vector.tensor_add(out=dist2[:], in0=row_gap[:], in1=col_gap[:])
+    adj = const.tile([P, TOKENS], F32)
+    nc.vector.tensor_single_scalar(out=adj[:], in_=dist2[:], scalar=2.0, op=ALU.is_le)
+    degree = const.tile([P, 1], F32)
+    nc.vector.reduce_sum(out=degree[:], in_=adj[:], axis=AXIS.X)
+    nc.vector.tensor_scalar_add(out=degree[:], in0=degree[:], scalar1=EPS_DEG)
+    root = const.tile([P, 1], F32)
+    nc.scalar.sqrt(out=root[:], in_=degree[:])
+    d = const.tile([P, 1], F32)
+    nc.vector.reciprocal(out=d[:], in_=root[:])
+    return adj, d
+
+
+def tile_graphconvolutionbatch_k_kernel(tc, H, W_words, W_scales, gamma, beta, out):
+    nc = tc.nc
+    h_rows = H.rearrange("b n k -> (b n) k")
+    out_rows = out.rearrange("b n f -> (b n) f")
+    w_rows = W_words.rearrange("g p n t -> p g (n t)")
+    whole_groups = GROUPS - SPLIT_GROUPS
+
+    with ExitStack() as ctx:
+        const = ctx.enter_context(tc.tile_pool(name="const", bufs=1))
+        keep = ctx.enter_context(tc.tile_pool(name="keep", bufs=1))
+        stage = ctx.enter_context(tc.tile_pool(name="stage", bufs=4))
+        psum = ctx.enter_context(tc.psum_pool(name="psum", bufs=1))
+
+        w_planes = keep.tile([P, GROUPS // PLANES_PER_TILE, FEATURES], U8, align_bytes=64)
+        nc.vector.memset(w_planes[:].rearrange("p a n -> p (a n)").bitcast(I32), 0)
+        gb_rows = const.tile([P, P], BF16)
+        nc.vector.memset(gb_rows[:], 0.0)
+        eps_col = const.tile([P, 1], F32)
+        nc.vector.memset(eps_col[:], EPS_BN)
+        ident = const.tile([P, P], F32)
+        masks.make_identity(nc, ident[:])
+        nc.scalar.dma_start(out=gb_rows[0:F_TILES, :], in_=gamma.rearrange("(j f) -> j f", f=P))
+        nc.scalar.dma_start(out=gb_rows[F_TILES : 2 * F_TILES, :], in_=beta.rearrange("(j f) -> j f", f=P))
+
+        h_tiles = []
+        for c in range(H_CHUNKS):
+            h_sb = keep.tile([P, GROUPS_PER_H_CHUNK * K_PASS], BF16, name="h%d" % c)
+            width = GROUPS_PER_H_CHUNK * K_PASS
+            nc.sync.dma_start(out=h_sb[:], in_=h_rows[:, c * width : (c + 1) * width])
+            h_tiles.append(h_sb)
+        for a in range(GROUPS // PLANES_PER_TILE):
+            for quadrant in range(4):
+                nc.sync.dma_start(
+                    out=w_planes[32 * quadrant : 32 * quadrant + 16, a, :].bitcast(I32),
+                    in_=W_scales[
+                        PLANES_PER_TILE * a : PLANES_PER_TILE * (a + 1), 4 * quadrant : 4 * quadrant + 4, :
+                    ].bitcast(I32),
+                )
+        w_words = {}
+        for first in range(0, whole_groups, W_GROUPS_PER_LOAD):
+            w_sb = keep.tile([P, W_GROUPS_PER_LOAD, FEATURES], U32, name="w%d" % first, align_bytes=64)
+            nc.sync.dma_start(
+                out=w_sb[:].bitcast(I32), in_=w_rows[:, first : first + W_GROUPS_PER_LOAD, :].bitcast(I32)
+            )
+            for i in range(W_GROUPS_PER_LOAD):
+                for half in range(2):
+                    w_words[(first + i, half)] = w_sb[:, i, half * HALF : (half + 1) * HALF]
+        for half in range(2):
+            for first in range(whole_groups, GROUPS, SPLIT_GROUPS_PER_LOAD):
+                w_sb = keep.tile(
+                    [P, SPLIT_GROUPS_PER_LOAD, HALF], U32, name="w%d_%d" % (first, half), align_bytes=64
+                )
+                nc.sync.dma_start(
+                    out=w_sb[:].bitcast(I32),
+                    in_=w_rows[
+                        :, first : first + SPLIT_GROUPS_PER_LOAD, 4 * half * HALF : 4 * (half + 1) * HALF
+                    ].bitcast(I32),
+                )
+                for i in range(SPLIT_GROUPS_PER_LOAD):
+                    w_words[(first + i, half)] = w_sb[:, i, :]
+
+        h_codes = keep.tile([P, GROUPS, TOKENS], U32, align_bytes=64)
+        h_scales = keep.tile([P, GROUPS, TOKENS], U8, align_bytes=64)
+        for pair in range(GROUPS // 2):
+            chunk, local = divmod(2 * pair, GROUPS_PER_H_CHUNK)
+            words = h_tiles[chunk][:].bitcast(F32)
+            flipped = psum.tile([P, 2, 2, TOKENS], F32, tag="bank%d" % (pair % BANKS))
+            for i in range(2):
+                first = (K_PASS // 2) * (local + i)
+                for u in range(2):
+                    nc.tensor.transpose(
+                        flipped[:, i, u, :], words[:, first + u : first + K_PASS // 2 : 2], ident[:]
+                    )
+            grouped = stage.tile([P, 2, TOKENS, 4], BF16, align_bytes=64)
+            nc.scalar.copy(out=grouped[:].bitcast(F32), in_=flipped[:].rearrange("p i u r -> p i r u"))
+            nc.vector.quantize_mx(
+                out=h_codes[:, 2 * pair : 2 * pair + 2, :].rearrange("p i r -> p (i r)").bitcast(FP8X4),
+                scales=h_scales[:, 2 * pair : 2 * pair + 2, :].rearrange("p i r -> p (i r)"),
+                in_=grouped[:].rearrange("p i r t -> p (i r t)"),
+            )
+
+        adj, d = build_grid_tables(nc, const, psum, ident)
+        gb_f32 = const.tile([P, P], F32)
+        nc.vector.tensor_copy(out=gb_f32[:], in_=gb_rows[:])
+        gb_ps = psum.tile([P, P], F32, tag="bank7")
+        nc.tensor.transpose(gb_ps[:], gb_f32[:], ident[:])
+        gb = const.tile([P, 2 * F_TILES], F32)
+        nc.vector.tensor_copy(out=gb[:], in_=gb_ps[:, 0 : 2 * F_TILES])
+        gamma_col = gb[:, 0:F_TILES]
+        beta_col = gb[:, F_TILES : 2 * F_TILES]
+
+        acc = []
+        for j in range(F_TILES):
+            acc_j = psum.tile([P, TOKENS], F32, tag="bank%d" % j, name="acc%d" % j)
+            acc.append(acc_j)
+
+        def multiply(g, half):
+            plane_start = 4 * (g % PLANES_PER_TILE)
+            for i in range(F_TILES // 2):
+                j = half * F_TILES // 2 + i
+                nc.tensor.matmul_mx(
+                    out=acc[j][:],
+                    lhsT=w_words[(g, half)][:, P * i : P * (i + 1)].bitcast(FP8X4),
+                    lhsT_scale=w_planes[plane_start:P, g // PLANES_PER_TILE, P * j : P * (j + 1)],
+                    rhs=h_codes[:, g, :].bitcast(FP8X4),
+                    rhs_scale=h_scales[:, g, :],
+                    start=(g == 0),
+                    stop=(g == GROUPS - 1),
+                )
+
+        stats = const.tile([P, F_TILES, 6], F32)
+        mean_var = const.tile([P, F_TILES, 2], F32)
+        std = const.tile([P, F_TILES], F32)
+        rstd = const.tile([P, F_TILES], F32)
+        gain = const.tile([P, F_TILES], F32)
+        mean_gain = const.tile([P, F_TILES], F32)
+        shift = const.tile([P, F_TILES], F32)
+        normed = const.tile([P, F_TILES, TOKENS], F32)
+        scaled = const.tile([P, FEATURES], F32)
+        result = const.tile([P, FEATURES], F32)
+
+        def tiles_of(half):
+            return range(half * F_TILES // 2, (half + 1) * F_TILES // 2)
+
+        def statistics(half):
+            for j in tiles_of(half):
+                nc.vector.bn_stats(out=stats[:, j, :], in_=acc[j][:])
+                nc.vector.bn_aggr(out=mean_var[:, j, :], in_=stats[:, j, :])
+
+        def gains(half):
+            js = slice(half * F_TILES // 2, (half + 1) * F_TILES // 2)
+            nc.scalar.activation(out=std[:, js], in_=mean_var[:, js, 1], func=ACT.Sqrt, bias=eps_col[:], scale=1.0)
+            nc.vector.reciprocal(out=rstd[:, js], in_=std[:, js])
+            nc.vector.tensor_mul(out=gain[:, js], in0=gamma_col[:, js], in1=rstd[:, js])
+            nc.vector.tensor_mul(out=mean_gain[:, js], in0=mean_var[:, js, 0], in1=gain[:, js])
+            nc.vector.tensor_sub(out=shift[:, js], in0=beta_col[:, js], in1=mean_gain[:, js])
+
+        def normalise(half):
+            for j in tiles_of(half):
+                if j % 2 == 0:
+                    nc.scalar.activation(
+                        out=normed[:, j, :], in_=acc[j][:], func=ACT.Identity,
+                        bias=shift[:, j : j + 1], scale=gain[:, j : j + 1],
+                    )
+                else:
+                    nc.vector.tensor_scalar(
+                        out=normed[:, j, :], in0=acc[j][:], scalar1=gain[:, j : j + 1],
+                        scalar2=shift[:, j : j + 1], op0=ALU.mult, op1=ALU.add,
+                    )
+
+        def on_scalar(half, quarter):
+            return half == 0 or quarter % 2 == 0
+
+        def to_tokens(half):
+            for quarter in range(2 * half, 2 * half + 2):
+                tokens_ps = psum.tile([P, 2 * P], F32, tag="bank%d" % (2 * quarter))
+                for i in range(2):
+                    nc.tensor.transpose(tokens_ps[:, P * i : P * (i + 1)], normed[:, 2 * quarter + i, :], ident[:])
+                cols = slice(2 * P * quarter, 2 * P * (quarter + 1))
+                if on_scalar(half, quarter):
+                    nc.scalar.activation(out=scaled[:, cols], in_=tokens_ps[:], func=ACT.Relu, scale=d[:])
+                else:
+                    nc.vector.tensor_scalar(
+                        out=scaled[:, cols], in0=tokens_ps[:], scalar1=d[:], scalar2=0.0, op0=ALU.mult, op1=ALU.max
+                    )
+
+        def neighbours(half):
+            for quarter in range(2 * half, 2 * half + 2):
+                cols = slice(2 * P * quarter, 2 * P * (quarter + 1))
+                summed = psum.tile([P, 2 * P], F32, tag="bank%d" % (2 * quarter + 1))
+                nc.tensor.matmul(summed[:], lhsT=adj[:], rhs=scaled[:, cols], start=True, stop=True)
+                if on_scalar(half, quarter):
+                    nc.scalar.activation(out=result[:, cols], in_=summed[:], func=ACT.Copy, scale=d[:])
+                else:
+                    nc.vector.tensor_scalar_mul(out=result[:, cols], in0=summed[:], scalar1=d[:])
+                nc.sync.dma_start(out=out_rows[:, cols], in_=result[:, cols])
+
+        for g in range(whole_groups):
+            multiply(g, 0)
+            multiply(g, 1)
+        for g in range(whole_groups, GROUPS):
+            multiply(g, 0)
+        statistics(0)
+        gains(0)
+        normalise(0)
+        for g in range(whole_groups, GROUPS):
+            multiply(g, 1)
+        to_tokens(0)
+        statistics(1)
+        gains(1)
+        neighbours(0)
+        normalise(1)
+        to_tokens(1)
+        neighbours(1)

@@ -91,20 +91,19 @@ def tile_graphconvolutionbatch_k_kernel(tc, H, W_words, W_scales, gamma, beta, o
         nc.scalar.dma_start(out=gb_rows[0:F_TILES, :], in_=gamma.rearrange("(j f) -> j f", f=P))
         nc.scalar.dma_start(out=gb_rows[F_TILES : 2 * F_TILES, :], in_=beta.rearrange("(j f) -> j f", f=P))
 
+        scale_rows = W_scales.rearrange("(a s) (c r) n -> s r c a n", s=PLANES_PER_TILE, r=4)
+        for s in range(PLANES_PER_TILE):
+            for r in range(4):
+                nc.gpsimd.dma_start(
+                    out=w_planes[4 * s + r : P : 32, :, :].bitcast(F32), in_=scale_rows[s, r].bitcast(F32)
+                )
+
         h_tiles = []
         for c in range(H_CHUNKS):
             h_sb = keep.tile([P, GROUPS_PER_H_CHUNK * K_PASS], BF16, name="h%d" % c)
             width = GROUPS_PER_H_CHUNK * K_PASS
             nc.sync.dma_start(out=h_sb[:], in_=h_rows[:, c * width : (c + 1) * width])
             h_tiles.append(h_sb)
-        for a in range(GROUPS // PLANES_PER_TILE):
-            for quadrant in range(4):
-                nc.sync.dma_start(
-                    out=w_planes[32 * quadrant : 32 * quadrant + 16, a, :].bitcast(I32),
-                    in_=W_scales[
-                        PLANES_PER_TILE * a : PLANES_PER_TILE * (a + 1), 4 * quadrant : 4 * quadrant + 4, :
-                    ].bitcast(I32),
-                )
         w_words = {}
         for first in range(0, whole_groups, W_GROUPS_PER_LOAD):
             w_sb = keep.tile([P, W_GROUPS_PER_LOAD, FEATURES], U32, name="w%d" % first, align_bytes=64)

@@ -28,6 +28,7 @@ SPLIT_GROUPS = 8
 HALF = FEATURES // 2
 SPLIT_GROUPS_PER_LOAD = 2
 PLANES_PER_TILE = 4
+SYNC_BLOCKS = 3
 EPS_BN = 1e-5
 EPS_DEG = 1e-5
 
@@ -88,15 +89,19 @@ def tile_graphconvolutionbatch_k_kernel(tc, H, W_words, W_scales, gamma, beta, o
         nc.vector.memset(eps_col[:], EPS_BN)
         ident = const.tile([P, P], F32)
         masks.make_identity(nc, ident[:])
+        adj, d = build_grid_tables(nc, const, psum, ident)
         nc.scalar.dma_start(out=gb_rows[0:F_TILES, :], in_=gamma.rearrange("(j f) -> j f", f=P))
         nc.scalar.dma_start(out=gb_rows[F_TILES : 2 * F_TILES, :], in_=beta.rearrange("(j f) -> j f", f=P))
 
-        scale_rows = W_scales.rearrange("(a s) (c r) n -> s r c a n", s=PLANES_PER_TILE, r=4)
-        for s in range(PLANES_PER_TILE):
-            for r in range(4):
-                nc.gpsimd.dma_start(
-                    out=w_planes[4 * s + r : P : 32, :, :].bitcast(F32), in_=scale_rows[s, r].bitcast(F32)
+        def load_scales(queue, view, a):
+            for c in range(4):
+                queue.dma_start(
+                    out=w_planes[32 * c : 32 * c + 16, a, :].bitcast(view),
+                    in_=W_scales[PLANES_PER_TILE * a : PLANES_PER_TILE * (a + 1), 4 * c : 4 * c + 4, :].bitcast(view),
                 )
+
+        for a in range(SYNC_BLOCKS, GROUPS // PLANES_PER_TILE):
+            load_scales(nc.gpsimd, F32, a)
 
         h_tiles = []
         for c in range(H_CHUNKS):
@@ -104,6 +109,8 @@ def tile_graphconvolutionbatch_k_kernel(tc, H, W_words, W_scales, gamma, beta, o
             width = GROUPS_PER_H_CHUNK * K_PASS
             nc.sync.dma_start(out=h_sb[:], in_=h_rows[:, c * width : (c + 1) * width])
             h_tiles.append(h_sb)
+        for a in range(SYNC_BLOCKS):
+            load_scales(nc.sync, I32, a)
         w_words = {}
         for first in range(0, whole_groups, W_GROUPS_PER_LOAD):
             w_sb = keep.tile([P, W_GROUPS_PER_LOAD, FEATURES], U32, name="w%d" % first, align_bytes=64)
@@ -147,7 +154,6 @@ def tile_graphconvolutionbatch_k_kernel(tc, H, W_words, W_scales, gamma, beta, o
                 in_=grouped[:].rearrange("p i r t -> p (i r t)"),
             )
 
-        adj, d = build_grid_tables(nc, const, psum, ident)
         gb_f32 = const.tile([P, P], F32)
         nc.vector.tensor_copy(out=gb_f32[:], in_=gb_rows[:])
         gb_ps = psum.tile([P, P], F32, tag="bank7")

@@ -25,10 +25,15 @@ H_CHUNKS = 4
 GROUPS_PER_H_CHUNK = GROUPS // H_CHUNKS
 W_GROUPS_PER_LOAD = 2
 SPLIT_GROUPS = 8
-HALF = FEATURES // 2
-SPLIT_GROUPS_PER_LOAD = 2
+SECTIONS = (range(0, 4), range(4, 6), range(6, 8))
+CHUNKS = (
+    ((range(0, 2), True, 0, 1), (range(2, 4), True, 2, 3)),
+    ((range(4, 6), True, 4, 5),),
+    ((range(6, 7), True, 0, 1), (range(7, 8), False, 2, 3)),
+)
+TOKENS_AFTER = 3
+NEIGHBOURS_AFTER = 5
 PLANES_PER_TILE = 4
-SYNC_BLOCKS = 3
 EPS_BN = 1e-5
 EPS_DEG = 1e-5
 
@@ -100,8 +105,6 @@ def tile_graphconvolutionbatch_k_kernel(tc, H, W_words, W_scales, gamma, beta, o
                     in_=W_scales[PLANES_PER_TILE * a : PLANES_PER_TILE * (a + 1), 4 * c : 4 * c + 4, :].bitcast(view),
                 )
 
-        for a in range(SYNC_BLOCKS, GROUPS // PLANES_PER_TILE):
-            load_scales(nc.gpsimd, F32, a)
 
         h_tiles = []
         for c in range(H_CHUNKS):
@@ -109,30 +112,29 @@ def tile_graphconvolutionbatch_k_kernel(tc, H, W_words, W_scales, gamma, beta, o
             width = GROUPS_PER_H_CHUNK * K_PASS
             nc.sync.dma_start(out=h_sb[:], in_=h_rows[:, c * width : (c + 1) * width])
             h_tiles.append(h_sb)
-        for a in range(SYNC_BLOCKS):
-            load_scales(nc.sync, I32, a)
+            load_scales(nc.sync, I32, c)
         w_words = {}
-        for first in range(0, whole_groups, W_GROUPS_PER_LOAD):
-            w_sb = keep.tile([P, W_GROUPS_PER_LOAD, FEATURES], U32, name="w%d" % first, align_bytes=64)
+
+        def load_w(first, tiles):
+            columns = slice(P * tiles.start, P * tiles.stop)
+            w_sb = keep.tile(
+                [P, W_GROUPS_PER_LOAD, P * len(tiles)], U32, name="w%d_%d" % (first, tiles.start), align_bytes=64
+            )
             nc.sync.dma_start(
-                out=w_sb[:].bitcast(I32), in_=w_rows[:, first : first + W_GROUPS_PER_LOAD, :].bitcast(I32)
+                out=w_sb[:].bitcast(I32),
+                in_=w_rows[:, first : first + W_GROUPS_PER_LOAD, 4 * columns.start : 4 * columns.stop].bitcast(I32),
             )
             for i in range(W_GROUPS_PER_LOAD):
-                for half in range(2):
-                    w_words[(first + i, half)] = w_sb[:, i, half * HALF : (half + 1) * HALF]
-        for half in range(2):
-            for first in range(whole_groups, GROUPS, SPLIT_GROUPS_PER_LOAD):
-                w_sb = keep.tile(
-                    [P, SPLIT_GROUPS_PER_LOAD, HALF], U32, name="w%d_%d" % (first, half), align_bytes=64
-                )
-                nc.sync.dma_start(
-                    out=w_sb[:].bitcast(I32),
-                    in_=w_rows[
-                        :, first : first + SPLIT_GROUPS_PER_LOAD, 4 * half * HALF : 4 * (half + 1) * HALF
-                    ].bitcast(I32),
-                )
-                for i in range(SPLIT_GROUPS_PER_LOAD):
-                    w_words[(first + i, half)] = w_sb[:, i, :]
+                for j in tiles:
+                    w_words[(first + i, j)] = w_sb[:, i, P * (j - tiles.start) : P * (j - tiles.start + 1)]
+
+        for first in range(0, whole_groups, W_GROUPS_PER_LOAD):
+            load_w(first, range(F_TILES))
+            if first // W_GROUPS_PER_LOAD < H_CHUNKS:
+                load_scales(nc.sync, I32, H_CHUNKS + first // W_GROUPS_PER_LOAD)
+        for tiles in SECTIONS:
+            for first in range(whole_groups, GROUPS, W_GROUPS_PER_LOAD):
+                load_w(first, tiles)
 
         h_codes = keep.tile([P, GROUPS, TOKENS], U32, align_bytes=64)
         h_scales = keep.tile([P, GROUPS, TOKENS], U8, align_bytes=64)
@@ -168,13 +170,12 @@ def tile_graphconvolutionbatch_k_kernel(tc, H, W_words, W_scales, gamma, beta, o
             acc_j = psum.tile([P, TOKENS], F32, tag="bank%d" % j, name="acc%d" % j)
             acc.append(acc_j)
 
-        def multiply(g, half):
+        def multiply(g, tiles):
             plane_start = 4 * (g % PLANES_PER_TILE)
-            for i in range(F_TILES // 2):
-                j = half * F_TILES // 2 + i
+            for j in tiles:
                 nc.tensor.matmul_mx(
                     out=acc[j][:],
-                    lhsT=w_words[(g, half)][:, P * i : P * (i + 1)].bitcast(FP8X4),
+                    lhsT=w_words[(g, j)].bitcast(FP8X4),
                     lhsT_scale=w_planes[plane_start:P, g // PLANES_PER_TILE, P * j : P * (j + 1)],
                     rhs=h_codes[:, g, :].bitcast(FP8X4),
                     rhs_scale=h_scales[:, g, :],
@@ -193,24 +194,21 @@ def tile_graphconvolutionbatch_k_kernel(tc, H, W_words, W_scales, gamma, beta, o
         scaled = const.tile([P, FEATURES], F32)
         result = const.tile([P, FEATURES], F32)
 
-        def tiles_of(half):
-            return range(half * F_TILES // 2, (half + 1) * F_TILES // 2)
-
-        def statistics(half):
-            for j in tiles_of(half):
+        def statistics(tiles):
+            for j in tiles:
                 nc.vector.bn_stats(out=stats[:, j, :], in_=acc[j][:])
                 nc.vector.bn_aggr(out=mean_var[:, j, :], in_=stats[:, j, :])
 
-        def gains(half):
-            js = slice(half * F_TILES // 2, (half + 1) * F_TILES // 2)
+        def gains(tiles):
+            js = slice(tiles.start, tiles.stop)
             nc.scalar.activation(out=std[:, js], in_=mean_var[:, js, 1], func=ACT.Sqrt, bias=eps_col[:], scale=1.0)
             nc.vector.reciprocal(out=rstd[:, js], in_=std[:, js])
             nc.vector.tensor_mul(out=gain[:, js], in0=gamma_col[:, js], in1=rstd[:, js])
             nc.vector.tensor_mul(out=mean_gain[:, js], in0=mean_var[:, js, 0], in1=gain[:, js])
             nc.vector.tensor_sub(out=shift[:, js], in0=beta_col[:, js], in1=mean_gain[:, js])
 
-        def normalise(half):
-            for j in tiles_of(half):
+        def normalise(tiles):
+            for j in tiles:
                 if j % 2 == 0:
                     nc.scalar.activation(
                         out=normed[:, j, :], in_=acc[j][:], func=ACT.Identity,
@@ -222,47 +220,41 @@ def tile_graphconvolutionbatch_k_kernel(tc, H, W_words, W_scales, gamma, beta, o
                         scalar2=shift[:, j : j + 1], op0=ALU.mult, op1=ALU.add,
                     )
 
-        def on_scalar(half, quarter):
-            return half == 0 or quarter % 2 == 0
-
-        def to_tokens(half):
-            for quarter in range(2 * half, 2 * half + 2):
-                tokens_ps = psum.tile([P, 2 * P], F32, tag="bank%d" % (2 * quarter))
-                for i in range(2):
-                    nc.tensor.transpose(tokens_ps[:, P * i : P * (i + 1)], normed[:, 2 * quarter + i, :], ident[:])
-                cols = slice(2 * P * quarter, 2 * P * (quarter + 1))
-                if on_scalar(half, quarter):
+        def to_tokens(section):
+            for tiles, on_scalar, bank, other in CHUNKS[section]:
+                cols = slice(P * tiles.start, P * tiles.stop)
+                tokens_ps = psum.tile([P, P * len(tiles)], F32, tag="bank%d" % bank)
+                for i, j in enumerate(tiles):
+                    nc.tensor.transpose(tokens_ps[:, P * i : P * (i + 1)], normed[:, j, :], ident[:])
+                if on_scalar:
                     nc.scalar.activation(out=scaled[:, cols], in_=tokens_ps[:], func=ACT.Relu, scale=d[:])
                 else:
                     nc.vector.tensor_scalar(
                         out=scaled[:, cols], in0=tokens_ps[:], scalar1=d[:], scalar2=0.0, op0=ALU.mult, op1=ALU.max
                     )
 
-        def neighbours(half):
-            for quarter in range(2 * half, 2 * half + 2):
-                cols = slice(2 * P * quarter, 2 * P * (quarter + 1))
-                summed = psum.tile([P, 2 * P], F32, tag="bank%d" % (2 * quarter + 1))
+        def neighbours(section):
+            for tiles, on_scalar, other, bank in CHUNKS[section]:
+                cols = slice(P * tiles.start, P * tiles.stop)
+                summed = psum.tile([P, P * len(tiles)], F32, tag="bank%d" % bank)
                 nc.tensor.matmul(summed[:], lhsT=adj[:], rhs=scaled[:, cols], start=True, stop=True)
-                if on_scalar(half, quarter):
+                if on_scalar:
                     nc.scalar.activation(out=result[:, cols], in_=summed[:], func=ACT.Copy, scale=d[:])
                 else:
                     nc.vector.tensor_scalar_mul(out=result[:, cols], in0=summed[:], scalar1=d[:])
                 nc.sync.dma_start(out=out_rows[:, cols], in_=result[:, cols])
 
         for g in range(whole_groups):
-            multiply(g, 0)
-            multiply(g, 1)
-        for g in range(whole_groups, GROUPS):
-            multiply(g, 0)
-        statistics(0)
-        gains(0)
-        normalise(0)
-        for g in range(whole_groups, GROUPS):
-            multiply(g, 1)
-        to_tokens(0)
-        statistics(1)
-        gains(1)
-        neighbours(0)
-        normalise(1)
-        to_tokens(1)
-        neighbours(1)
+            multiply(g, range(F_TILES))
+        for s, tiles in enumerate(SECTIONS):
+            for i in range(SPLIT_GROUPS):
+                multiply(whole_groups + i, tiles)
+                if s > 0 and i == TOKENS_AFTER:
+                    to_tokens(s - 1)
+                if s > 0 and i == NEIGHBOURS_AFTER:
+                    neighbours(s - 1)
+            statistics(tiles)
+            gains(tiles)
+            normalise(tiles)
+        to_tokens(len(SECTIONS) - 1)
+        neighbours(len(SECTIONS) - 1)

@@ -24,18 +24,26 @@ BANKS = 8
 H_CHUNKS = 4
 GROUPS_PER_H_CHUNK = GROUPS // H_CHUNKS
 W_GROUPS_PER_LOAD = 2
-SPLIT_GROUPS = 8
+W_STRETCHES = (
+    (range(0, 8), range(0, 26, 2)),
+    (range(0, 4), range(26, 32, 2)),
+    (range(4, 8), range(26, 28, 2)),
+    (range(4, 6), range(28, 32, 2)),
+    (range(6, 8), range(28, 32, 2)),
+)
 SECTIONS = (range(0, 4), range(4, 6), range(6, 8))
 CHUNKS = (
-    ((range(0, 2), True, 0, 1), (range(2, 4), True, 2, 3)),
-    ((range(4, 6), True, 4, 5),),
-    ((range(6, 7), True, 0, 1), (range(7, 8), False, 2, 3)),
+    ((range(0, 2), 0, True, 1, True), (range(2, 4), 2, True, 3, True)),
+    ((range(4, 6), 4, False, 5, True),),
+    ((range(6, 7), 0, True, 1, True), (range(7, 8), 2, False, 3, False)),
 )
-TOKENS_AFTER = 3
-NEIGHBOURS_AFTER = 5
 PLANES_PER_TILE = 4
+SYNC_SCALES_AFTER = [6, 12]
+SYNC_BLOCKS = len(SYNC_SCALES_AFTER)
+SCALE_BLOCKS = GROUPS // PLANES_PER_TILE
 EPS_BN = 1e-5
 EPS_DEG = 1e-5
+LEAST_GAMMA2 = 1e-30
 
 FLOPS = 2 * TOKENS * K * FEATURES
 
@@ -66,10 +74,8 @@ def build_grid_tables(nc, const, psum, ident):
     degree = const.tile([P, 1], F32)
     nc.vector.reduce_sum(out=degree[:], in_=adj[:], axis=AXIS.X)
     nc.vector.tensor_scalar_add(out=degree[:], in0=degree[:], scalar1=EPS_DEG)
-    root = const.tile([P, 1], F32)
-    nc.scalar.sqrt(out=root[:], in_=degree[:])
     d = const.tile([P, 1], F32)
-    nc.vector.reciprocal(out=d[:], in_=root[:])
+    nc.scalar.activation(out=d[:], in_=degree[:], func=ACT.Abs_reciprocal_sqrt)
     return adj, d
 
 
@@ -78,7 +84,6 @@ def tile_graphconvolutionbatch_k_kernel(tc, H, W_words, W_scales, gamma, beta, o
     h_rows = H.rearrange("b n k -> (b n) k")
     out_rows = out.rearrange("b n f -> (b n) f")
     w_rows = W_words.rearrange("g p n t -> p g (n t)")
-    whole_groups = GROUPS - SPLIT_GROUPS
 
     with ExitStack() as ctx:
         const = ctx.enter_context(tc.tile_pool(name="const", bufs=1))
@@ -87,16 +92,13 @@ def tile_graphconvolutionbatch_k_kernel(tc, H, W_words, W_scales, gamma, beta, o
         psum = ctx.enter_context(tc.psum_pool(name="psum", bufs=1))
 
         w_planes = keep.tile([P, GROUPS // PLANES_PER_TILE, FEATURES], U8, align_bytes=64)
-        nc.vector.memset(w_planes[:].rearrange("p a n -> p (a n)").bitcast(I32), 0)
+        for a in range(SCALE_BLOCKS):
+            nc.vector.memset(w_planes[:, a, :].bitcast(I32), 0)
         gb_rows = const.tile([P, P], BF16)
         nc.vector.memset(gb_rows[:], 0.0)
-        eps_col = const.tile([P, 1], F32)
-        nc.vector.memset(eps_col[:], EPS_BN)
         ident = const.tile([P, P], F32)
         masks.make_identity(nc, ident[:])
         adj, d = build_grid_tables(nc, const, psum, ident)
-        nc.scalar.dma_start(out=gb_rows[0:F_TILES, :], in_=gamma.rearrange("(j f) -> j f", f=P))
-        nc.scalar.dma_start(out=gb_rows[F_TILES : 2 * F_TILES, :], in_=beta.rearrange("(j f) -> j f", f=P))
 
         def load_scales(queue, view, a):
             for c in range(4):
@@ -106,13 +108,17 @@ def tile_graphconvolutionbatch_k_kernel(tc, H, W_words, W_scales, gamma, beta, o
                 )
 
 
+        for a in range(SCALE_BLOCKS - SYNC_BLOCKS):
+            load_scales(nc.gpsimd, F32, a)
+
         h_tiles = []
         for c in range(H_CHUNKS):
             h_sb = keep.tile([P, GROUPS_PER_H_CHUNK * K_PASS], BF16, name="h%d" % c)
             width = GROUPS_PER_H_CHUNK * K_PASS
-            nc.sync.dma_start(out=h_sb[:], in_=h_rows[:, c * width : (c + 1) * width])
+            nc.scalar.dma_start(out=h_sb[:], in_=h_rows[:, c * width : (c + 1) * width])
             h_tiles.append(h_sb)
-            load_scales(nc.sync, I32, c)
+        nc.scalar.dma_start(out=gb_rows[0:F_TILES, :], in_=gamma.rearrange("(j f) -> j f", f=P))
+        nc.scalar.dma_start(out=gb_rows[F_TILES : 2 * F_TILES, :], in_=beta.rearrange("(j f) -> j f", f=P))
         w_words = {}
 
         def load_w(first, tiles):
@@ -128,13 +134,11 @@ def tile_graphconvolutionbatch_k_kernel(tc, H, W_words, W_scales, gamma, beta, o
                 for j in tiles:
                     w_words[(first + i, j)] = w_sb[:, i, P * (j - tiles.start) : P * (j - tiles.start + 1)]
 
-        for first in range(0, whole_groups, W_GROUPS_PER_LOAD):
-            load_w(first, range(F_TILES))
-            if first // W_GROUPS_PER_LOAD < H_CHUNKS:
-                load_scales(nc.sync, I32, H_CHUNKS + first // W_GROUPS_PER_LOAD)
-        for tiles in SECTIONS:
-            for first in range(whole_groups, GROUPS, W_GROUPS_PER_LOAD):
+        for tiles, groups in W_STRETCHES:
+            for first in groups:
                 load_w(first, tiles)
+                if first in SYNC_SCALES_AFTER:
+                    load_scales(nc.sync, I32, SCALE_BLOCKS - SYNC_BLOCKS + SYNC_SCALES_AFTER.index(first))
 
         h_codes = keep.tile([P, GROUPS, TOKENS], U32, align_bytes=64)
         h_scales = keep.tile([P, GROUPS, TOKENS], U8, align_bytes=64)
@@ -163,6 +167,19 @@ def tile_graphconvolutionbatch_k_kernel(tc, H, W_words, W_scales, gamma, beta, o
         gb = const.tile([P, 2 * F_TILES], F32)
         nc.vector.tensor_copy(out=gb[:], in_=gb_ps[:, 0 : 2 * F_TILES])
         gamma_col = gb[:, 0:F_TILES]
+        above = const.tile([P, F_TILES], F32)
+        below = const.tile([P, F_TILES], F32)
+        sign = const.tile([P, F_TILES], F32)
+        gamma2 = const.tile([P, F_TILES], F32)
+        inv_gamma2 = const.tile([P, F_TILES], F32)
+        eps_over_gamma2 = const.tile([P, F_TILES], F32)
+        nc.vector.tensor_single_scalar(out=above[:], in_=gamma_col, scalar=0.0, op=ALU.is_gt)
+        nc.vector.tensor_single_scalar(out=below[:], in_=gamma_col, scalar=0.0, op=ALU.is_lt)
+        nc.vector.tensor_sub(out=sign[:], in0=above[:], in1=below[:])
+        nc.vector.tensor_mul(out=gamma2[:], in0=gamma_col, in1=gamma_col)
+        nc.vector.tensor_scalar_max(out=gamma2[:], in0=gamma2[:], scalar1=LEAST_GAMMA2)
+        nc.vector.reciprocal(out=inv_gamma2[:], in_=gamma2[:])
+        nc.vector.tensor_scalar_mul(out=eps_over_gamma2[:], in0=inv_gamma2[:], scalar1=EPS_BN)
         beta_col = gb[:, F_TILES : 2 * F_TILES]
 
         acc = []
@@ -185,11 +202,8 @@ def tile_graphconvolutionbatch_k_kernel(tc, H, W_words, W_scales, gamma, beta, o
 
         stats = const.tile([P, F_TILES, 6], F32)
         mean_var = const.tile([P, F_TILES, 2], F32)
-        std = const.tile([P, F_TILES], F32)
-        rstd = const.tile([P, F_TILES], F32)
         gain = const.tile([P, F_TILES], F32)
-        mean_gain = const.tile([P, F_TILES], F32)
-        shift = const.tile([P, F_TILES], F32)
+        centred = const.tile([P, F_TILES, TOKENS], F32)
         normed = const.tile([P, F_TILES, TOKENS], F32)
         scaled = const.tile([P, FEATURES], F32)
         result = const.tile([P, FEATURES], F32)
@@ -197,31 +211,36 @@ def tile_graphconvolutionbatch_k_kernel(tc, H, W_words, W_scales, gamma, beta, o
         def statistics(tiles):
             for j in tiles:
                 nc.vector.bn_stats(out=stats[:, j, :], in_=acc[j][:])
+            for j in tiles:
                 nc.vector.bn_aggr(out=mean_var[:, j, :], in_=stats[:, j, :])
 
         def gains(tiles):
-            js = slice(tiles.start, tiles.stop)
-            nc.scalar.activation(out=std[:, js], in_=mean_var[:, js, 1], func=ACT.Sqrt, bias=eps_col[:], scale=1.0)
-            nc.vector.reciprocal(out=rstd[:, js], in_=std[:, js])
-            nc.vector.tensor_mul(out=gain[:, js], in0=gamma_col[:, js], in1=rstd[:, js])
-            nc.vector.tensor_mul(out=mean_gain[:, js], in0=mean_var[:, js, 0], in1=gain[:, js])
-            nc.vector.tensor_sub(out=shift[:, js], in0=beta_col[:, js], in1=mean_gain[:, js])
+            for j in tiles:
+                nc.scalar.activation(
+                    out=gain[:, j : j + 1], in_=mean_var[:, j, 1:2], func=ACT.Abs_reciprocal_sqrt,
+                    bias=eps_over_gamma2[:, j : j + 1], scale=inv_gamma2[:, j : j + 1],
+                )
+            for j in tiles:
+                nc.vector.tensor_scalar(
+                    out=centred[:, j, :], in0=acc[j][:], scalar1=mean_var[:, j, 0:1],
+                    scalar2=sign[:, j : j + 1], op0=ALU.subtract, op1=ALU.mult,
+                )
 
         def normalise(tiles):
             for j in tiles:
                 if j % 2 == 0:
                     nc.scalar.activation(
-                        out=normed[:, j, :], in_=acc[j][:], func=ACT.Identity,
-                        bias=shift[:, j : j + 1], scale=gain[:, j : j + 1],
+                        out=normed[:, j, :], in_=centred[:, j, :], func=ACT.Identity,
+                        bias=beta_col[:, j : j + 1], scale=gain[:, j : j + 1],
                     )
                 else:
                     nc.vector.tensor_scalar(
-                        out=normed[:, j, :], in0=acc[j][:], scalar1=gain[:, j : j + 1],
-                        scalar2=shift[:, j : j + 1], op0=ALU.mult, op1=ALU.add,
+                        out=normed[:, j, :], in0=centred[:, j, :], scalar1=gain[:, j : j + 1],
+                        scalar2=beta_col[:, j : j + 1], op0=ALU.mult, op1=ALU.add,
                     )
 
         def to_tokens(section):
-            for tiles, on_scalar, bank, other in CHUNKS[section]:
+            for tiles, bank, on_scalar, sum_bank, sum_on_scalar in CHUNKS[section]:
                 cols = slice(P * tiles.start, P * tiles.stop)
                 tokens_ps = psum.tile([P, P * len(tiles)], F32, tag="bank%d" % bank)
                 for i, j in enumerate(tiles):
@@ -233,28 +252,63 @@ def tile_graphconvolutionbatch_k_kernel(tc, H, W_words, W_scales, gamma, beta, o
                         out=scaled[:, cols], in0=tokens_ps[:], scalar1=d[:], scalar2=0.0, op0=ALU.mult, op1=ALU.max
                     )
 
-        def neighbours(section):
-            for tiles, on_scalar, other, bank in CHUNKS[section]:
-                cols = slice(P * tiles.start, P * tiles.stop)
+        sums = {}
+
+        def sum_neighbours(chunks):
+            for chunk in chunks:
+                tiles, token_bank, tokens_on_scalar, bank, on_scalar = chunk
                 summed = psum.tile([P, P * len(tiles)], F32, tag="bank%d" % bank)
+                cols = slice(P * tiles.start, P * tiles.stop)
                 nc.tensor.matmul(summed[:], lhsT=adj[:], rhs=scaled[:, cols], start=True, stop=True)
+                sums[chunk] = summed
+
+        def store_neighbours(chunks):
+            for chunk in chunks:
+                tiles, token_bank, tokens_on_scalar, bank, on_scalar = chunk
+                cols = slice(P * tiles.start, P * tiles.stop)
+                summed = sums[chunk]
                 if on_scalar:
                     nc.scalar.activation(out=result[:, cols], in_=summed[:], func=ACT.Copy, scale=d[:])
                 else:
                     nc.vector.tensor_scalar_mul(out=result[:, cols], in0=summed[:], scalar1=d[:])
                 nc.sync.dma_start(out=out_rows[:, cols], in_=result[:, cols])
 
-        for g in range(whole_groups):
-            multiply(g, range(F_TILES))
-        for s, tiles in enumerate(SECTIONS):
-            for i in range(SPLIT_GROUPS):
-                multiply(whole_groups + i, tiles)
-                if s > 0 and i == TOKENS_AFTER:
-                    to_tokens(s - 1)
-                if s > 0 and i == NEIGHBOURS_AFTER:
-                    neighbours(s - 1)
-            statistics(tiles)
-            gains(tiles)
-            normalise(tiles)
-        to_tokens(len(SECTIONS) - 1)
-        neighbours(len(SECTIONS) - 1)
+        def multiply_load(tiles, first):
+            for j in tiles:
+                for g in range(first, first + W_GROUPS_PER_LOAD):
+                    multiply(g, range(j, j + 1))
+
+        def norm(section):
+            statistics(SECTIONS[section])
+            gains(SECTIONS[section])
+            normalise(SECTIONS[section])
+
+        for stretch in range(2):
+            tiles, groups = W_STRETCHES[stretch]
+            for first in groups:
+                multiply_load(tiles, first)
+        norm(0)
+        tiles, groups = W_STRETCHES[2]
+        for first in groups:
+            multiply_load(tiles, first)
+        with tc.manual_schedule(
+            engines={mybir.EngineType.PE, mybir.EngineType.DVE, mybir.EngineType.Activation}
+        ):
+            tiles, groups = W_STRETCHES[3]
+            multiply_load(tiles, groups[0])
+            multiply_load(tiles, groups[1])
+            to_tokens(0)
+            tiles, groups = W_STRETCHES[4]
+            multiply_load(tiles, groups[0])
+            norm(1)
+            multiply_load(tiles, groups[1])
+            sum_neighbours(CHUNKS[0])
+            store_neighbours(CHUNKS[0][:1])
+            norm(2)
+            store_neighbours(CHUNKS[0][1:])
+            to_tokens(1)
+            to_tokens(2)
+            sum_neighbours(CHUNKS[1])
+            store_neighbours(CHUNKS[1])
+            sum_neighbours(CHUNKS[2])
+            store_neighbours(CHUNKS[2])

from contextlib import ExitStack

import concourse.masks as masks
import concourse.mybir as mybir

F32 = mybir.dt.float32
BF16 = mybir.dt.bfloat16
I32 = mybir.dt.int32
U32 = mybir.dt.uint32
U8 = mybir.dt.uint8
FP8X4 = mybir.dt.float8_e4m3fn_x4
ALU = mybir.AluOpType
ACT = mybir.ActivationFunctionType
AXIS = mybir.AxisListType

P = 128
TOKENS = 128
K = 16384
FEATURES = 1024
K_PASS = 512
GROUPS = K // K_PASS
F_TILES = FEATURES // P
BANKS = 8
H_CHUNKS = 4
GROUPS_PER_H_CHUNK = GROUPS // H_CHUNKS
W_GROUPS_PER_LOAD = 2
W_STRETCHES = (
    (range(0, 8), range(0, 26, 2)),
    (range(0, 4), range(26, 32, 2)),
    (range(4, 8), range(26, 28, 2)),
    (range(4, 6), range(28, 32, 2)),
    (range(6, 8), range(28, 32, 2)),
)
SECTIONS = (range(0, 4), range(4, 6), range(6, 8))
CHUNKS = (
    ((range(0, 2), 0, True, 1, True), (range(2, 4), 2, True, 3, True)),
    ((range(4, 6), 4, False, 5, True),),
    ((range(6, 7), 0, True, 1, True), (range(7, 8), 2, False, 3, False)),
)
PLANES_PER_TILE = 4
SYNC_SCALES_AFTER = [6, 12]
SYNC_BLOCKS = len(SYNC_SCALES_AFTER)
SCALE_BLOCKS = GROUPS // PLANES_PER_TILE
EPS_BN = 1e-5
EPS_DEG = 1e-5
LEAST_GAMMA2 = 1e-30

FLOPS = 2 * TOKENS * K * FEATURES


def build_grid_tables(nc, const, psum, ident):
    row_int = const.tile([P, TOKENS], I32)
    col_int = const.tile([P, TOKENS], I32)
    nc.gpsimd.iota(row_int[:], pattern=[[9, 2], [1, 8], [0, 8]], base=0, channel_multiplier=0)
    nc.gpsimd.iota(col_int[:], pattern=[[0, 16], [1, 8]], base=0, channel_multiplier=0)
    row_free = const.tile([P, TOKENS], F32)
    col_free = const.tile([P, TOKENS], F32)
    nc.vector.tensor_copy(out=row_free[:], in_=row_int[:])
    nc.vector.tensor_copy(out=col_free[:], in_=col_int[:])
    row_own = psum.tile([P, TOKENS], F32, tag="bank5")
    col_own = psum.tile([P, TOKENS], F32, tag="bank6")
    nc.tensor.transpose(row_own[:], row_free[:], ident[:])
    nc.tensor.transpose(col_own[:], col_free[:], ident[:])
    row_gap = const.tile([P, TOKENS], F32)
    col_gap = const.tile([P, TOKENS], F32)
    nc.vector.tensor_sub(out=row_gap[:], in0=row_free[:], in1=row_own[:])
    nc.vector.tensor_sub(out=col_gap[:], in0=col_free[:], in1=col_own[:])
    nc.vector.tensor_mul(out=row_gap[:], in0=row_gap[:], in1=row_gap[:])
    nc.vector.tensor_mul(out=col_gap[:], in0=col_gap[:], in1=col_gap[:])
    dist2 = const.tile([P, TOKENS], F32)
    nc.vector.tensor_add(out=dist2[:], in0=row_gap[:], in1=col_gap[:])
    adj = const.tile([P, TOKENS], F32)
    nc.vector.tensor_single_scalar(out=adj[:], in_=dist2[:], scalar=2.0, op=ALU.is_le)
    degree = const.tile([P, 1], F32)
    nc.vector.reduce_sum(out=degree[:], in_=adj[:], axis=AXIS.X)
    nc.vector.tensor_scalar_add(out=degree[:], in0=degree[:], scalar1=EPS_DEG)
    d = const.tile([P, 1], F32)
    nc.scalar.activation(out=d[:], in_=degree[:], func=ACT.Abs_reciprocal_sqrt)
    return adj, d


def tile_graphconvolutionbatch_k_kernel(tc, H, W_words, W_scales, gamma, beta, out):
    nc = tc.nc
    h_rows = H.rearrange("b n k -> (b n) k")
    out_rows = out.rearrange("b n f -> (b n) f")
    w_rows = W_words.rearrange("g p n t -> p g (n t)")

    with ExitStack() as ctx:
        const = ctx.enter_context(tc.tile_pool(name="const", bufs=1))
        keep = ctx.enter_context(tc.tile_pool(name="keep", bufs=1))
        stage = ctx.enter_context(tc.tile_pool(name="stage", bufs=4))
        psum = ctx.enter_context(tc.psum_pool(name="psum", bufs=1))

        w_planes = keep.tile([P, GROUPS // PLANES_PER_TILE, FEATURES], U8, align_bytes=64)
        for a in range(SCALE_BLOCKS):
            nc.vector.memset(w_planes[:, a, :].bitcast(I32), 0)
        gb_rows = const.tile([P, P], BF16)
        nc.vector.memset(gb_rows[:], 0.0)
        ident = const.tile([P, P], F32)
        masks.make_identity(nc, ident[:])
        adj, d = build_grid_tables(nc, const, psum, ident)

        def load_scales(queue, view, a):
            for c in range(4):
                queue.dma_start(
                    out=w_planes[32 * c : 32 * c + 16, a, :].bitcast(view),
                    in_=W_scales[PLANES_PER_TILE * a : PLANES_PER_TILE * (a + 1), 4 * c : 4 * c + 4, :].bitcast(view),
                )


        for a in range(SCALE_BLOCKS - SYNC_BLOCKS):
            load_scales(nc.gpsimd, F32, a)

        h_tiles = []
        for c in range(H_CHUNKS):
            h_sb = keep.tile([P, GROUPS_PER_H_CHUNK * K_PASS], BF16, name="h%d" % c)
            width = GROUPS_PER_H_CHUNK * K_PASS
            nc.scalar.dma_start(out=h_sb[:], in_=h_rows[:, c * width : (c + 1) * width])
            h_tiles.append(h_sb)
        nc.scalar.dma_start(out=gb_rows[0:F_TILES, :], in_=gamma.rearrange("(j f) -> j f", f=P))
        nc.scalar.dma_start(out=gb_rows[F_TILES : 2 * F_TILES, :], in_=beta.rearrange("(j f) -> j f", f=P))
        w_words = {}

        def load_w(first, tiles):
            columns = slice(P * tiles.start, P * tiles.stop)
            w_sb = keep.tile(
                [P, W_GROUPS_PER_LOAD, P * len(tiles)], U32, name="w%d_%d" % (first, tiles.start), align_bytes=64
            )
            nc.sync.dma_start(
                out=w_sb[:].bitcast(I32),
                in_=w_rows[:, first : first + W_GROUPS_PER_LOAD, 4 * columns.start : 4 * columns.stop].bitcast(I32),
            )
            for i in range(W_GROUPS_PER_LOAD):
                for j in tiles:
                    w_words[(first + i, j)] = w_sb[:, i, P * (j - tiles.start) : P * (j - tiles.start + 1)]

        for tiles, groups in W_STRETCHES:
            for first in groups:
                load_w(first, tiles)
                if first in SYNC_SCALES_AFTER:
                    load_scales(nc.sync, I32, SCALE_BLOCKS - SYNC_BLOCKS + SYNC_SCALES_AFTER.index(first))

        h_codes = keep.tile([P, GROUPS, TOKENS], U32, align_bytes=64)
        h_scales = keep.tile([P, GROUPS, TOKENS], U8, align_bytes=64)
        for pair in range(GROUPS // 2):
            chunk, local = divmod(2 * pair, GROUPS_PER_H_CHUNK)
            words = h_tiles[chunk][:].bitcast(F32)
            flipped = psum.tile([P, 2, 2, TOKENS], F32, tag="bank%d" % (pair % BANKS))
            for i in range(2):
                first = (K_PASS // 2) * (local + i)
                for u in range(2):
                    nc.tensor.transpose(
                        flipped[:, i, u, :], words[:, first + u : first + K_PASS // 2 : 2], ident[:]
                    )
            grouped = stage.tile([P, 2, TOKENS, 4], BF16, align_bytes=64)
            nc.scalar.copy(out=grouped[:].bitcast(F32), in_=flipped[:].rearrange("p i u r -> p i r u"))
            nc.vector.quantize_mx(
                out=h_codes[:, 2 * pair : 2 * pair + 2, :].rearrange("p i r -> p (i r)").bitcast(FP8X4),
                scales=h_scales[:, 2 * pair : 2 * pair + 2, :].rearrange("p i r -> p (i r)"),
                in_=grouped[:].rearrange("p i r t -> p (i r t)"),
            )

        gb_f32 = const.tile([P, P], F32)
        nc.vector.tensor_copy(out=gb_f32[:], in_=gb_rows[:])
        gb_ps = psum.tile([P, P], F32, tag="bank7")
        nc.tensor.transpose(gb_ps[:], gb_f32[:], ident[:])
        gb = const.tile([P, 2 * F_TILES], F32)
        nc.vector.tensor_copy(out=gb[:], in_=gb_ps[:, 0 : 2 * F_TILES])
        gamma_col = gb[:, 0:F_TILES]
        above = const.tile([P, F_TILES], F32)
        below = const.tile([P, F_TILES], F32)
        sign = const.tile([P, F_TILES], F32)
        gamma2 = const.tile([P, F_TILES], F32)
        inv_gamma2 = const.tile([P, F_TILES], F32)
        eps_over_gamma2 = const.tile([P, F_TILES], F32)
        nc.vector.tensor_single_scalar(out=above[:], in_=gamma_col, scalar=0.0, op=ALU.is_gt)
        nc.vector.tensor_single_scalar(out=below[:], in_=gamma_col, scalar=0.0, op=ALU.is_lt)
        nc.vector.tensor_sub(out=sign[:], in0=above[:], in1=below[:])
        nc.vector.tensor_mul(out=gamma2[:], in0=gamma_col, in1=gamma_col)
        nc.vector.tensor_scalar_max(out=gamma2[:], in0=gamma2[:], scalar1=LEAST_GAMMA2)
        nc.vector.reciprocal(out=inv_gamma2[:], in_=gamma2[:])
        nc.vector.tensor_scalar_mul(out=eps_over_gamma2[:], in0=inv_gamma2[:], scalar1=EPS_BN)
        beta_col = gb[:, F_TILES : 2 * F_TILES]

        acc = []
        for j in range(F_TILES):
            acc_j = psum.tile([P, TOKENS], F32, tag="bank%d" % j, name="acc%d" % j)
            acc.append(acc_j)

        def multiply(g, tiles):
            plane_start = 4 * (g % PLANES_PER_TILE)
            for j in tiles:
                nc.tensor.matmul_mx(
                    out=acc[j][:],
                    lhsT=w_words[(g, j)].bitcast(FP8X4),
                    lhsT_scale=w_planes[plane_start:P, g // PLANES_PER_TILE, P * j : P * (j + 1)],
                    rhs=h_codes[:, g, :].bitcast(FP8X4),
                    rhs_scale=h_scales[:, g, :],
                    start=(g == 0),
                    stop=(g == GROUPS - 1),
                )

        stats = const.tile([P, F_TILES, 6], F32)
        mean_var = const.tile([P, F_TILES, 2], F32)
        gain = const.tile([P, F_TILES], F32)
        centred = const.tile([P, F_TILES, TOKENS], F32)
        normed = const.tile([P, F_TILES, TOKENS], F32)
        scaled = const.tile([P, FEATURES], F32)
        result = const.tile([P, FEATURES], F32)

        def statistics(tiles):
            for j in tiles:
                nc.vector.bn_stats(out=stats[:, j, :], in_=acc[j][:])
            for j in tiles:
                nc.vector.bn_aggr(out=mean_var[:, j, :], in_=stats[:, j, :])

        def gains(tiles):
            for j in tiles:
                nc.scalar.activation(
                    out=gain[:, j : j + 1], in_=mean_var[:, j, 1:2], func=ACT.Abs_reciprocal_sqrt,
                    bias=eps_over_gamma2[:, j : j + 1], scale=inv_gamma2[:, j : j + 1],
                )
            for j in tiles:
                nc.vector.tensor_scalar(
                    out=centred[:, j, :], in0=acc[j][:], scalar1=mean_var[:, j, 0:1],
                    scalar2=sign[:, j : j + 1], op0=ALU.subtract, op1=ALU.mult,
                )

        def normalise(tiles):
            for j in tiles:
                if j % 2 == 0:
                    nc.scalar.activation(
                        out=normed[:, j, :], in_=centred[:, j, :], func=ACT.Identity,
                        bias=beta_col[:, j : j + 1], scale=gain[:, j : j + 1],
                    )
                else:
                    nc.vector.tensor_scalar(
                        out=normed[:, j, :], in0=centred[:, j, :], scalar1=gain[:, j : j + 1],
                        scalar2=beta_col[:, j : j + 1], op0=ALU.mult, op1=ALU.add,
                    )

        def to_tokens(section):
            for tiles, bank, on_scalar, sum_bank, sum_on_scalar in CHUNKS[section]:
                cols = slice(P * tiles.start, P * tiles.stop)
                tokens_ps = psum.tile([P, P * len(tiles)], F32, tag="bank%d" % bank)
                for i, j in enumerate(tiles):
                    nc.tensor.transpose(tokens_ps[:, P * i : P * (i + 1)], normed[:, j, :], ident[:])
                if on_scalar:
                    nc.scalar.activation(out=scaled[:, cols], in_=tokens_ps[:], func=ACT.Relu, scale=d[:])
                else:
                    nc.vector.tensor_scalar(
                        out=scaled[:, cols], in0=tokens_ps[:], scalar1=d[:], scalar2=0.0, op0=ALU.mult, op1=ALU.max
                    )

        sums = {}

        def sum_neighbours(chunks):
            for chunk in chunks:
                tiles, token_bank, tokens_on_scalar, bank, on_scalar = chunk
                summed = psum.tile([P, P * len(tiles)], F32, tag="bank%d" % bank)
                cols = slice(P * tiles.start, P * tiles.stop)
                nc.tensor.matmul(summed[:], lhsT=adj[:], rhs=scaled[:, cols], start=True, stop=True)
                sums[chunk] = summed

        def store_neighbours(chunks):
            for chunk in chunks:
                tiles, token_bank, tokens_on_scalar, bank, on_scalar = chunk
                cols = slice(P * tiles.start, P * tiles.stop)
                summed = sums[chunk]
                if on_scalar:
                    nc.scalar.activation(out=result[:, cols], in_=summed[:], func=ACT.Copy, scale=d[:])
                else:
                    nc.vector.tensor_scalar_mul(out=result[:, cols], in0=summed[:], scalar1=d[:])
                nc.sync.dma_start(out=out_rows[:, cols], in_=result[:, cols])

        def multiply_load(tiles, first):
            for j in tiles:
                for g in range(first, first + W_GROUPS_PER_LOAD):
                    multiply(g, range(j, j + 1))

        def norm(section):
            statistics(SECTIONS[section])
            gains(SECTIONS[section])
            normalise(SECTIONS[section])

        for stretch in range(2):
            tiles, groups = W_STRETCHES[stretch]
            for first in groups:
                multiply_load(tiles, first)
        norm(0)
        tiles, groups = W_STRETCHES[2]
        for first in groups:
            multiply_load(tiles, first)
        with tc.manual_schedule(
            engines={mybir.EngineType.PE, mybir.EngineType.DVE, mybir.EngineType.Activation}
        ):
            tiles, groups = W_STRETCHES[3]
            multiply_load(tiles, groups[0])
            multiply_load(tiles, groups[1])
            to_tokens(0)
            tiles, groups = W_STRETCHES[4]
            multiply_load(tiles, groups[0])
            norm(1)
            multiply_load(tiles, groups[1])
            sum_neighbours(CHUNKS[0])
            store_neighbours(CHUNKS[0][:1])
            norm(2)
            store_neighbours(CHUNKS[0][1:])
            to_tokens(1)
            to_tokens(2)
            sum_neighbours(CHUNKS[1])
            store_neighbours(CHUNKS[1])
            sum_neighbours(CHUNKS[2])
            store_neighbours(CHUNKS[2])
